import numpy as np
import ml_dtypes


def mxq(x, axis, fmt="e4m3"):
    dtype, down = {"e4m3": (ml_dtypes.float8_e4m3fn, 7), "e5m2": (ml_dtypes.float8_e5m2, 14)}[fmt]
    v = np.moveaxis(np.asarray(x, np.float32).astype(ml_dtypes.bfloat16).astype(np.float64), axis, -1)
    blocks = v.reshape(v.shape[:-1] + (-1, 32))
    amax = np.abs(blocks).max(-1, keepdims=True)
    byte = np.maximum(np.where(amax > 0, np.frexp(amax)[1] - 1 + 127, 0) - down, 1)
    scale = np.exp2(byte - 127.0)
    codes = (blocks / scale).astype(np.float32).astype(dtype).astype(np.float64)
    return np.moveaxis((codes * scale).reshape(v.shape), -1, axis)


WIDE = False


def mx_kscale(k):
    if not WIDE:
        return np.ones(k)
    levels = np.array([10, -10, 5, -5, 0])
    a = np.random.permutation(np.resize(levels, k // 512 * 4)).reshape(k // 512, 4)
    idx = np.arange(k)
    return np.exp2(a[idx // 512, idx % 128 // 32])


BF16 = ml_dtypes.bfloat16


def bf(x):
    return np.asarray(x, np.float32).astype(BF16)


def f64(x):
    return np.asarray(x).astype(np.float64)


BATCH, ROWS, COLS, IN_DIM, OUT_DIM = 2, 64, 64, 512, 512
N = ROWS * COLS
EPS_BN = 1e-5
EPS_DEG = 1e-5


def _stencil9(x):
    R, C = x.shape[-3], x.shape[-2]
    pad = [(0, 0)] * (x.ndim - 3) + [(1, 1), (1, 1), (0, 0)]
    xp = np.pad(x, pad)
    out = np.zeros_like(x)
    for di in range(3):
        for dj in range(3):
            out = out + xp[..., di:di + R, dj:dj + C, :]
    return out


def _deg_inv_sqrt(rows, cols):
    D = _stencil9(np.ones((rows, cols, 1)))[..., 0]
    return (D + EPS_DEG) ** -0.5


def setup_inputs():
    s = mx_kscale(IN_DIM)
    mu = 0.5 * np.random.standard_normal(IN_DIM)
    bound = np.sqrt(6.0 / IN_DIM)
    return {"H": bf((np.random.standard_normal((BATCH, N, IN_DIM)) + mu) * s),
            "W": bf(np.random.uniform(-bound, bound, (IN_DIM, OUT_DIM)) / s[:, None]),
            "gamma": bf(1.0 + 0.1 * np.random.standard_normal(OUT_DIM)),
            "beta": bf(0.2 * np.random.standard_normal(OUT_DIM))}


def reference(H, W, gamma, beta):
    B, n_nodes, _ = H.shape
    Ht = mxq(f64(H), 2, "e4m3") @ mxq(f64(W), 0, "e4m3")
    mean = Ht.mean(axis=(0, 1))
    var = Ht.var(axis=(0, 1))
    Ht = (Ht - mean) * (1.0 / np.sqrt(var + EPS_BN)) * f64(gamma) + f64(beta)
    Ht = np.maximum(Ht, 0.0)
    d = _deg_inv_sqrt(ROWS, COLS)[None, :, :, None]
    Hg = Ht.reshape(B, ROWS, COLS, OUT_DIM)
    Hagg = d * _stencil9(Hg * d)
    return Hagg.reshape(B, n_nodes, OUT_DIM)

@@ -1,0 +1,249 @@
+from contextlib import ExitStack
+
+import concourse.mybir as mybir
+from concourse.masks import make_identity
+
+F32 = mybir.dt.float32
+BF16 = mybir.dt.bfloat16
+U32 = mybir.dt.uint32
+U8 = mybir.dt.uint8
+FP8X4 = mybir.dt.float8_e4m3fn_x4
+ACT = mybir.ActivationFunctionType
+ALU = mybir.AluOpType
+AXIS = mybir.AxisListType
+
+P = 128
+BATCH, ROWS, COLS = 2, 64, 64
+IN_DIM, OUT_DIM = 512, 512
+NODES = BATCH * ROWS * COLS
+EPS_BN = 1e-5
+EPS_DEG = 1e-5
+
+PACK = 4
+F_BLOCKS = OUT_DIM // P
+CHUNK_COLS = 4
+CHUNK = CHUNK_COLS * P
+N_CHUNKS = COLS // CHUNK_COLS
+RUNS = CHUNK // ROWS
+PITCH = 72
+FIRST = 4
+N_PADDED = 3
+
+D9 = (9.0 + EPS_DEG) ** -0.5
+D6 = (6.0 + EPS_DEG) ** -0.5
+D4 = (4.0 + EPS_DEG) ** -0.5
+
+FLOPS = 2 * NODES * IN_DIM * OUT_DIM
+
+
+def column_runs(chunk):
+    if chunk == 0:
+        return [(0, 1, True), (1, CHUNK_COLS - 1, False)]
+    if chunk == N_CHUNKS - 1:
+        return [(0, CHUNK_COLS - 1, False), (CHUNK_COLS - 1, 1, True)]
+    return [(0, CHUNK_COLS, False)]
+
+
+def tile_graphconvolutionbatch_kernel(tc, H, W, gamma, beta, out):
+    nc = tc.nc
+    h_view = H.rearrange("b (r c) k -> (b r) c k", c=COLS)
+    out_view = out.rearrange("b (r c) f -> (b r) c f", c=COLS)
+
+    with ExitStack() as ctx:
+        const = ctx.enter_context(tc.tile_pool(name="const", bufs=1))
+        loads = ctx.enter_context(tc.tile_pool(name="loads", bufs=6))
+        stage = ctx.enter_context(tc.tile_pool(name="stage", bufs=3))
+        sums = ctx.enter_context(tc.tile_pool(name="sums", bufs=4))
+        stores = ctx.enter_context(tc.tile_pool(name="stores", bufs=3))
+        psum = ctx.enter_context(tc.psum_pool(name="psum", bufs=4))
+
+        ident = const.tile([P, P], F32)
+        make_identity(nc, ident[:])
+
+        w_raw = const.tile([P, PACK, OUT_DIM], BF16)
+        for u in range(2):
+            nc.sync.dma_start(
+                out=w_raw[:, 2 * u : 2 * u + 2, :],
+                in_=W[256 * u : 256 * (u + 1), :].rearrange("(q e) f -> q e f", e=2),
+            )
+        w_grouped = const.tile([P, OUT_DIM, PACK], BF16, align_bytes=64)
+        nc.vector.tensor_copy(out=w_grouped[:], in_=w_raw[:].rearrange("p t f -> p f t"))
+        w_codes = const.tile([P, OUT_DIM], U32, align_bytes=64)
+        w_scales = const.tile([P, OUT_DIM], U8, align_bytes=64)
+        nc.vector.quantize_mx(
+            out=w_codes[:].bitcast(FP8X4),
+            scales=w_scales[:],
+            in_=w_grouped[:].rearrange("p f t -> p (f t)"),
+        )
+
+        gb_rows = const.tile([P, P], BF16)
+        nc.vector.memset(gb_rows[:], 0.0)
+        nc.scalar.dma_start(out=gb_rows[0:F_BLOCKS, :], in_=gamma.rearrange("(j p) -> j p", p=P))
+        nc.scalar.dma_start(
+            out=gb_rows[F_BLOCKS : 2 * F_BLOCKS, :], in_=beta.rearrange("(j p) -> j p", p=P)
+        )
+        gb_rows_f32 = const.tile([P, P], F32)
+        nc.vector.tensor_copy(out=gb_rows_f32[:], in_=gb_rows[:])
+        gb_bank = psum.tile([P, P], F32, tag="t")
+        nc.tensor.transpose(gb_bank[:], gb_rows_f32[:], ident[:])
+        gb = const.tile([P, 2 * F_BLOCKS], F32)
+        nc.vector.tensor_copy(out=gb[:], in_=gb_bank[:, 0 : 2 * F_BLOCKS])
+
+        on_row_edge = const.tile([P, 1], F32)
+        nc.vector.tensor_reduce(
+            out=on_row_edge[:],
+            in_=ident[:].rearrange("p (b r) -> p b r", r=ROWS)[:, :, 0 : ROWS : ROWS - 1],
+            axis=AXIS.XY,
+            op=ALU.add,
+        )
+        rows_in_reach = const.tile([P, 1], F32)
+        nc.vector.tensor_scalar(
+            out=rows_in_reach[:], in0=on_row_edge[:], scalar1=-1.0, scalar2=3.0, op0=ALU.mult, op1=ALU.add
+        )
+        degree = const.tile([P, COLS], F32)
+        nc.vector.memset(degree[:], 3.0)
+        nc.vector.memset(degree[:, 0 : COLS : COLS - 1], 2.0)
+        nc.vector.tensor_scalar(
+            out=degree[:], in0=degree[:], scalar1=rows_in_reach[:, 0:1], scalar2=EPS_DEG, op0=ALU.mult, op1=ALU.add
+        )
+        nc.scalar.sqrt(out=degree[:], in_=degree[:])
+        d_out = const.tile([P, COLS], F32)
+        nc.vector.reciprocal(out=d_out[:], in_=degree[:])
+
+        padded = []
+        for i in range(N_PADDED):
+            pad_tile = const.tile([P, F_BLOCKS, RUNS, PITCH], F32, name="padded%d" % i)
+            nc.vector.memset(pad_tile[:, :, :, FIRST - 1 : FIRST + ROWS + 1 : ROWS + 1], 0.0)
+            padded.append(pad_tile)
+
+        h_codes = const.tile([P, NODES], U32, align_bytes=64)
+        h_scales = const.tile([P, NODES], U8, align_bytes=64)
+        stats = const.tile([P, F_BLOCKS, N_CHUNKS, 6], F32)
+
+        def multiply(chunk, fb):
+            nodes = slice(chunk * CHUNK, (chunk + 1) * CHUNK)
+            feats = slice(fb * P, (fb + 1) * P)
+            y = psum.tile([P, CHUNK], F32, tag="y")
+            nc.tensor.matmul_mx(
+                out=y[:],
+                lhsT=w_codes[:, feats].bitcast(FP8X4),
+                lhsT_scale=w_scales[:, feats],
+                rhs=h_codes[:, nodes].bitcast(FP8X4),
+                rhs_scale=h_scales[:, nodes],
+                start=True,
+                stop=True,
+            )
+            return y
+
+        for chunk in range(N_CHUNKS):
+            h_raw = loads.tile([P, CHUNK_COLS, IN_DIM], BF16)
+            nc.sync.dma_start(
+                out=h_raw[:], in_=h_view[:, chunk * CHUNK_COLS : (chunk + 1) * CHUNK_COLS, :]
+            )
+            grouped = stage.tile([P, CHUNK * PACK], BF16, align_bytes=64)
+            grouped_words = grouped[:].bitcast(F32).rearrange("p (n u) -> p n u", u=2)
+            for half in range(2):
+                turned = psum.tile([P, 2, 2 * P], F32, tag="t")
+                for i in range(2):
+                    words = h_raw[:, 2 * half + i, :].bitcast(F32)
+                    for u in range(2):
+                        nc.tensor.transpose(
+                            turned[:, u, i * P : (i + 1) * P], words[:, u * P : (u + 1) * P], ident[:]
+                        )
+                nc.scalar.copy(
+                    out=grouped_words[:, half * 2 * P : (half + 1) * 2 * P, :],
+                    in_=turned[:].rearrange("p u n -> p n u"),
+                )
+            nodes = slice(chunk * CHUNK, (chunk + 1) * CHUNK)
+            nc.vector.quantize_mx(
+                out=h_codes[:, nodes].bitcast(FP8X4), scales=h_scales[:, nodes], in_=grouped[:]
+            )
+            for fb in range(F_BLOCKS):
+                y = multiply(chunk, fb)
+                nc.vector.bn_stats(out=stats[:, fb, chunk, :], in_=y[:])
+
+        mean_var = const.tile([P, F_BLOCKS, 2], F32)
+        for fb in range(F_BLOCKS):
+            nc.vector.bn_aggr(out=mean_var[:, fb, :], in_=stats[:, fb, :, :].rearrange("p j s -> p (j s)"))
+        std = const.tile([P, F_BLOCKS], F32)
+        nc.vector.tensor_scalar_add(out=std[:], in0=mean_var[:, :, 1], scalar1=EPS_BN)
+        nc.scalar.sqrt(out=std[:], in_=std[:])
+        rstd = const.tile([P, F_BLOCKS], F32)
+        nc.vector.reciprocal(out=rstd[:], in_=std[:])
+        gain_shift = const.tile([P, 2, F_BLOCKS], F32)
+        nc.vector.tensor_mul(out=gain_shift[:, 0, :], in0=gb[:, 0:F_BLOCKS], in1=rstd[:])
+        mean_gain = const.tile([P, F_BLOCKS], F32)
+        nc.vector.tensor_mul(out=mean_gain[:], in0=mean_var[:, :, 0], in1=gain_shift[:, 0, :])
+        nc.vector.tensor_sub(out=gain_shift[:, 1, :], in0=gb[:, F_BLOCKS : 2 * F_BLOCKS], in1=mean_gain[:])
+        inner = const.tile([P, 2, F_BLOCKS], F32)
+        nc.vector.tensor_scalar_mul(out=inner[:], in0=gain_shift[:], scalar1=D9)
+        edge = const.tile([P, 2, F_BLOCKS], F32)
+        nc.vector.tensor_scalar_mul(out=edge[:], in0=gain_shift[:], scalar1=D6)
+
+        row_sums = {}
+        results = {}
+
+        def sum_over_rows(chunk):
+            pad_tile = padded[chunk % N_PADDED]
+            for fb in range(F_BLOCKS):
+                y = multiply(chunk, fb)
+                y_runs = y[:].rearrange("p (q r) -> p q r", r=ROWS)
+                for first, count, on_edge in column_runs(chunk):
+                    runs = slice(BATCH * first, BATCH * (first + count))
+                    coeff = edge if on_edge else inner
+                    nc.scalar.activation(
+                        out=pad_tile[:, fb, runs, FIRST : FIRST + ROWS],
+                        in_=y_runs[:, runs, :],
+                        func=ACT.Relu,
+                        bias=coeff[:, 1, fb : fb + 1],
+                        scale=coeff[:, 0, fb : fb + 1],
+                    )
+            for first, count, on_edge in column_runs(chunk):
+                runs = slice(BATCH * first, BATCH * (first + count))
+                ends = pad_tile[:, :, runs, FIRST : FIRST + ROWS : ROWS - 1]
+                nc.vector.tensor_scalar_mul(out=ends, in0=ends, scalar1=(D4 / D6 if on_edge else D6 / D9))
+            total = sums.tile([P, F_BLOCKS, CHUNK], F32, name="total")
+            total_runs = total[:].rearrange("p f (q r) -> p f q r", r=ROWS)
+            nc.vector.tensor_add(
+                out=total_runs,
+                in0=pad_tile[:, :, :, FIRST - 1 : FIRST - 1 + ROWS],
+                in1=pad_tile[:, :, :, FIRST + 1 : FIRST + 1 + ROWS],
+            )
+            nc.vector.tensor_add(
+                out=total_runs, in0=total_runs, in1=pad_tile[:, :, :, FIRST : FIRST + ROWS]
+            )
+            row_sums[chunk] = total
+
+        def finish_column(c):
+            taps = [cc for cc in (c - 1, c, c + 1) if 0 <= cc < COLS]
+            turned_back = psum.tile([P, OUT_DIM], F32, tag="t")
+            for fb in range(F_BLOCKS):
+                for i, cc in enumerate(taps):
+                    at = (cc % CHUNK_COLS) * P
+                    nc.tensor.matmul(
+                        out=turned_back[:, fb * P : (fb + 1) * P],
+                        lhsT=row_sums[cc // CHUNK_COLS][:, fb, at : at + P],
+                        rhs=ident[:],
+                        is_transpose=True,
+                        start=(i == 0),
+                        stop=(i == len(taps) - 1),
+                    )
+            group = c // CHUNK_COLS
+            if c % CHUNK_COLS == 0:
+                results[group] = stores.tile([P, CHUNK_COLS, OUT_DIM], F32, name="result")
+            nc.scalar.activation(
+                out=results[group][:, c % CHUNK_COLS, :],
+                in_=turned_back[:],
+                func=ACT.Copy,
+                scale=d_out[:, c : c + 1],
+            )
+            if c % CHUNK_COLS == CHUNK_COLS - 1:
+                nc.sync.dma_start(
+                    out=out_view[:, group * CHUNK_COLS : (group + 1) * CHUNK_COLS, :], in_=results[group][:]
+                )
+
+        for chunk in range(N_CHUNKS):
+            sum_over_rows(chunk)
+            for c in range(max(chunk * CHUNK_COLS - 1, 0), (chunk + 1) * CHUNK_COLS - 1):
+                finish_column(c)
+        finish_column(COLS - 1)

@@ -28,6 +28,10 @@ RUNS = CHUNK // ROWS
 PITCH = 72
 FIRST = 4
 N_PADDED = 3
+LOAD_BUFS = 6
+AHEAD = 2
+STEP = 2
+LAG = 8
 
 D9 = (9.0 + EPS_DEG) ** -0.5
 D6 = (6.0 + EPS_DEG) ** -0.5
@@ -51,11 +55,19 @@ def tile_graphconvolutionbatch_kernel(tc, H, W, gamma, beta, out):
 
     with ExitStack() as ctx:
         const = ctx.enter_context(tc.tile_pool(name="const", bufs=1))
-        loads = ctx.enter_context(tc.tile_pool(name="loads", bufs=6))
+        loads = ctx.enter_context(tc.tile_pool(name="loads", bufs=LOAD_BUFS))
         stage = ctx.enter_context(tc.tile_pool(name="stage", bufs=3))
-        sums = ctx.enter_context(tc.tile_pool(name="sums", bufs=4))
+        sums = ctx.enter_context(tc.tile_pool(name="sums", bufs=5))
         stores = ctx.enter_context(tc.tile_pool(name="stores", bufs=3))
         psum = ctx.enter_context(tc.psum_pool(name="psum", bufs=4))
+
+        h_raw = {}
+
+        def load(chunk):
+            h_raw[chunk] = loads.tile([P, CHUNK_COLS, IN_DIM], BF16, name="h_raw")
+            nc.sync.dma_start(
+                out=h_raw[chunk][:], in_=h_view[:, chunk * CHUNK_COLS : (chunk + 1) * CHUNK_COLS, :]
+            )
 
         ident = const.tile([P, P], F32)
         make_identity(nc, ident[:])
@@ -66,6 +78,8 @@ def tile_graphconvolutionbatch_kernel(tc, H, W, gamma, beta, out):
                 out=w_raw[:, 2 * u : 2 * u + 2, :],
                 in_=W[256 * u : 256 * (u + 1), :].rearrange("(q e) f -> q e f", e=2),
             )
+        for chunk in range(LOAD_BUFS):
+            load(chunk)
         w_grouped = const.tile([P, OUT_DIM, PACK], BF16, align_bytes=64)
         nc.vector.tensor_copy(out=w_grouped[:], in_=w_raw[:].rearrange("p t f -> p f t"))
         w_codes = const.tile([P, OUT_DIM], U32, align_bytes=64)
@@ -135,17 +149,13 @@ def tile_graphconvolutionbatch_kernel(tc, H, W, gamma, beta, out):
             )
             return y
 
-        for chunk in range(N_CHUNKS):
-            h_raw = loads.tile([P, CHUNK_COLS, IN_DIM], BF16)
-            nc.sync.dma_start(
-                out=h_raw[:], in_=h_view[:, chunk * CHUNK_COLS : (chunk + 1) * CHUNK_COLS, :]
-            )
-            grouped = stage.tile([P, CHUNK * PACK], BF16, align_bytes=64)
+        def turn(chunk):
+            grouped = stage.tile([P, CHUNK * PACK], BF16, align_bytes=64, name="grouped")
             grouped_words = grouped[:].bitcast(F32).rearrange("p (n u) -> p n u", u=2)
             for half in range(2):
-                turned = psum.tile([P, 2, 2 * P], F32, tag="t")
+                turned = psum.tile([P, 2, 2 * P], F32, tag="t", name="turned")
                 for i in range(2):
-                    words = h_raw[:, 2 * half + i, :].bitcast(F32)
+                    words = h_raw[chunk][:, 2 * half + i, :].bitcast(F32)
                     for u in range(2):
                         nc.tensor.transpose(
                             turned[:, u, i * P : (i + 1) * P], words[:, u * P : (u + 1) * P], ident[:]
@@ -154,13 +164,29 @@ def tile_graphconvolutionbatch_kernel(tc, H, W, gamma, beta, out):
                     out=grouped_words[:, half * 2 * P : (half + 1) * 2 * P, :],
                     in_=turned[:].rearrange("p u n -> p n u"),
                 )
+            return grouped
+
+        def quantise(chunk, grouped):
             nodes = slice(chunk * CHUNK, (chunk + 1) * CHUNK)
             nc.vector.quantize_mx(
                 out=h_codes[:, nodes].bitcast(FP8X4), scales=h_scales[:, nodes], in_=grouped[:]
             )
+
+        ctx.enter_context(tc.manual_schedule())
+
+        def prepare(chunk):
+            quantise(chunk, turn(chunk))
+            if chunk + LOAD_BUFS < N_CHUNKS:
+                load(chunk + LOAD_BUFS)
+
+        for chunk in range(AHEAD):
+            prepare(chunk)
+        for chunk in range(N_CHUNKS):
             for fb in range(F_BLOCKS):
                 y = multiply(chunk, fb)
                 nc.vector.bn_stats(out=stats[:, fb, chunk, :], in_=y[:])
+            if chunk + AHEAD < N_CHUNKS:
+                prepare(chunk + AHEAD)
 
         mean_var = const.tile([P, F_BLOCKS, 2], F32)
         for fb in range(F_BLOCKS):
@@ -183,21 +209,23 @@ def tile_graphconvolutionbatch_kernel(tc, H, W, gamma, beta, out):
         row_sums = {}
         results = {}
 
+        def norm_relu(chunk, fb):
+            pad_tile = padded[chunk % N_PADDED]
+            y = multiply(chunk, fb)
+            y_runs = y[:].rearrange("p (q r) -> p q r", r=ROWS)
+            for first, count, on_edge in column_runs(chunk):
+                runs = slice(BATCH * first, BATCH * (first + count))
+                coeff = edge if on_edge else inner
+                nc.scalar.activation(
+                    out=pad_tile[:, fb, runs, FIRST : FIRST + ROWS],
+                    in_=y_runs[:, runs, :],
+                    func=ACT.Relu,
+                    bias=coeff[:, 1, fb : fb + 1],
+                    scale=coeff[:, 0, fb : fb + 1],
+                )
+
         def sum_over_rows(chunk):
             pad_tile = padded[chunk % N_PADDED]
-            for fb in range(F_BLOCKS):
-                y = multiply(chunk, fb)
-                y_runs = y[:].rearrange("p (q r) -> p q r", r=ROWS)
-                for first, count, on_edge in column_runs(chunk):
-                    runs = slice(BATCH * first, BATCH * (first + count))
-                    coeff = edge if on_edge else inner
-                    nc.scalar.activation(
-                        out=pad_tile[:, fb, runs, FIRST : FIRST + ROWS],
-                        in_=y_runs[:, runs, :],
-                        func=ACT.Relu,
-                        bias=coeff[:, 1, fb : fb + 1],
-                        scale=coeff[:, 0, fb : fb + 1],
-                    )
             for first, count, on_edge in column_runs(chunk):
                 runs = slice(BATCH * first, BATCH * (first + count))
                 ends = pad_tile[:, :, runs, FIRST : FIRST + ROWS : ROWS - 1]
@@ -242,8 +270,11 @@ def tile_graphconvolutionbatch_kernel(tc, H, W, gamma, beta, out):
                     out=out_view[:, group * CHUNK_COLS : (group + 1) * CHUNK_COLS, :], in_=results[group][:]
                 )
 
-        for chunk in range(N_CHUNKS):
-            sum_over_rows(chunk)
-            for c in range(max(chunk * CHUNK_COLS - 1, 0), (chunk + 1) * CHUNK_COLS - 1):
+        n_passes = N_CHUNKS * F_BLOCKS
+        for first_pass in range(0, n_passes + LAG, STEP):
+            for m in range(first_pass, min(first_pass + STEP, n_passes)):
+                norm_relu(m // F_BLOCKS, m % F_BLOCKS)
+                if m % F_BLOCKS == F_BLOCKS - 1:
+                    sum_over_rows(m // F_BLOCKS)
+            for c in range(max(first_pass - LAG, 0), min(first_pass - LAG + STEP, COLS)):
                 finish_column(c)
-        finish_column(COLS - 1)

@@ -25,8 +25,10 @@ CHUNK_COLS = 4
 CHUNK = CHUNK_COLS * P
 N_CHUNKS = COLS // CHUNK_COLS
 RUNS = CHUNK // ROWS
+HALF = ROWS // 2
 PITCH = 72
-FIRST = 4
+ODD_AT = 4
+EVEN_AT = ODD_AT + HALF
 N_PADDED = 3
 LOAD_BUFS = 6
 AHEAD = 2
@@ -58,6 +60,8 @@ def tile_graphconvolutionbatch_kernel(tc, H, W, gamma, beta, out):
         loads = ctx.enter_context(tc.tile_pool(name="loads", bufs=LOAD_BUFS))
         stage = ctx.enter_context(tc.tile_pool(name="stage", bufs=3))
         sums = ctx.enter_context(tc.tile_pool(name="sums", bufs=5))
+        halves = ctx.enter_context(tc.tile_pool(name="halves", bufs=2))
+        pairs = ctx.enter_context(tc.tile_pool(name="pairs", bufs=5))
         stores = ctx.enter_context(tc.tile_pool(name="stores", bufs=3))
         psum = ctx.enter_context(tc.psum_pool(name="psum", bufs=4))
 
@@ -71,6 +75,11 @@ def tile_graphconvolutionbatch_kernel(tc, H, W, gamma, beta, out):
 
         ident = const.tile([P, P], F32)
         make_identity(nc, ident[:])
+        odd_first = const.tile([P, P], F32)
+        ident_rows = ident[:].rearrange("p (b k t) -> p b t k", b=BATCH, t=2)
+        odd_first_halves = odd_first[:].rearrange("p (b s k) -> p b s k", b=BATCH, s=2)
+        for s in range(2):
+            nc.vector.tensor_copy(out=odd_first_halves[:, :, s, :], in_=ident_rows[:, :, 1 - s, :])
 
         w_raw = const.tile([P, PACK, OUT_DIM], BF16)
         for u in range(2):
@@ -126,8 +135,8 @@ def tile_graphconvolutionbatch_kernel(tc, H, W, gamma, beta, out):
 
         padded = []
         for i in range(N_PADDED):
-            pad_tile = const.tile([P, F_BLOCKS, RUNS, PITCH], F32, name="padded%d" % i)
-            nc.vector.memset(pad_tile[:, :, :, FIRST - 1 : FIRST + ROWS + 1 : ROWS + 1], 0.0)
+            pad_tile = const.tile([P, F_BLOCKS * RUNS, PITCH], F32, name="padded%d" % i)
+            nc.vector.memset(pad_tile[:, :, ODD_AT - 1 : ODD_AT + ROWS + 1 : ROWS + 1], 0.0)
             padded.append(pad_tile)
 
         h_codes = const.tile([P, NODES], U32, align_bytes=64)
@@ -158,7 +167,7 @@ def tile_graphconvolutionbatch_kernel(tc, H, W, gamma, beta, out):
                     words = h_raw[chunk][:, 2 * half + i, :].bitcast(F32)
                     for u in range(2):
                         nc.tensor.transpose(
-                            turned[:, u, i * P : (i + 1) * P], words[:, u * P : (u + 1) * P], ident[:]
+                            turned[:, u, i * P : (i + 1) * P], words[:, u * P : (u + 1) * P], odd_first[:]
                         )
                 nc.scalar.copy(
                     out=grouped_words[:, half * 2 * P : (half + 1) * 2 * P, :],
@@ -207,6 +216,7 @@ def tile_graphconvolutionbatch_kernel(tc, H, W, gamma, beta, out):
         nc.vector.tensor_scalar_mul(out=edge[:], in0=gain_shift[:], scalar1=D6)
 
         row_sums = {}
+        pair_sums = {}
         results = {}
 
         def norm_relu(chunk, fb):
@@ -214,11 +224,10 @@ def tile_graphconvolutionbatch_kernel(tc, H, W, gamma, beta, out):
             y = multiply(chunk, fb)
             y_runs = y[:].rearrange("p (q r) -> p q r", r=ROWS)
             for first, count, on_edge in column_runs(chunk):
-                runs = slice(BATCH * first, BATCH * (first + count))
                 coeff = edge if on_edge else inner
                 nc.scalar.activation(
-                    out=pad_tile[:, fb, runs, FIRST : FIRST + ROWS],
-                    in_=y_runs[:, runs, :],
+                    out=pad_tile[:, fb * RUNS + BATCH * first : fb * RUNS + BATCH * (first + count), ODD_AT : ODD_AT + ROWS],
+                    in_=y_runs[:, BATCH * first : BATCH * (first + count), :],
                     func=ACT.Relu,
                     bias=coeff[:, 1, fb : fb + 1],
                     scale=coeff[:, 0, fb : fb + 1],
@@ -226,35 +235,50 @@ def tile_graphconvolutionbatch_kernel(tc, H, W, gamma, beta, out):
 
         def sum_over_rows(chunk):
             pad_tile = padded[chunk % N_PADDED]
+            by_block = pad_tile[:].rearrange("p (f q) s -> p f q s", f=F_BLOCKS)
             for first, count, on_edge in column_runs(chunk):
-                runs = slice(BATCH * first, BATCH * (first + count))
-                ends = pad_tile[:, :, runs, FIRST : FIRST + ROWS : ROWS - 1]
+                ends = by_block[:, :, BATCH * first : BATCH * (first + count), EVEN_AT - 1 : EVEN_AT + 1]
                 nc.vector.tensor_scalar_mul(out=ends, in0=ends, scalar1=(D4 / D6 if on_edge else D6 / D9))
-            total = sums.tile([P, F_BLOCKS, CHUNK], F32, name="total")
-            total_runs = total[:].rearrange("p f (q r) -> p f q r", r=ROWS)
+            both = halves.tile([P, F_BLOCKS * RUNS, HALF], F32, name="both")
             nc.vector.tensor_add(
-                out=total_runs,
-                in0=pad_tile[:, :, :, FIRST - 1 : FIRST - 1 + ROWS],
-                in1=pad_tile[:, :, :, FIRST + 1 : FIRST + 1 + ROWS],
+                out=both[:],
+                in0=pad_tile[:, :, EVEN_AT : EVEN_AT + HALF],
+                in1=pad_tile[:, :, ODD_AT : ODD_AT + HALF],
             )
+            outer = (
+                pad_tile[:, :, ODD_AT - 1 : ODD_AT - 1 + 2 * (HALF + 2)]
+                .rearrange("p g (t w) -> p g t w", t=2)[:, :, :, 0:HALF]
+                .rearrange("p g t k -> p g k t")
+            )
+            total = sums.tile([P, F_BLOCKS, CHUNK], F32, name="total")
             nc.vector.tensor_add(
-                out=total_runs, in0=total_runs, in1=pad_tile[:, :, :, FIRST : FIRST + ROWS]
+                out=total[:].rearrange("p f (q k t) -> p (f q) k t", k=HALF, t=2),
+                in0=both[:].unsqueeze(3).to_broadcast([P, F_BLOCKS * RUNS, HALF, 2]),
+                in1=outer,
             )
             row_sums[chunk] = total
+            pair = pairs.tile([P, F_BLOCKS, CHUNK // 2], F32, name="pair")
+            columns = total[:].rearrange("p f (e two n) -> p (f e) two n", two=2, n=P)
+            nc.vector.tensor_add(
+                out=pair[:].rearrange("p f (e n) -> p (f e) n", n=P), in0=columns[:, :, 0, :], in1=columns[:, :, 1, :]
+            )
+            pair_sums[chunk] = pair
 
         def finish_column(c):
-            taps = [cc for cc in (c - 1, c, c + 1) if 0 <= cc < COLS]
+            beyond = c - 1 if c % 2 == 0 else c + 1
+            parts = [(pair_sums[c // CHUNK_COLS], (c % CHUNK_COLS) // 2)]
+            if 0 <= beyond < COLS:
+                parts.append((row_sums[beyond // CHUNK_COLS], beyond % CHUNK_COLS))
             turned_back = psum.tile([P, OUT_DIM], F32, tag="t")
-            for fb in range(F_BLOCKS):
-                for i, cc in enumerate(taps):
-                    at = (cc % CHUNK_COLS) * P
+            for i, (source, col) in enumerate(parts):
+                for fb in range(F_BLOCKS):
                     nc.tensor.matmul(
                         out=turned_back[:, fb * P : (fb + 1) * P],
-                        lhsT=row_sums[cc // CHUNK_COLS][:, fb, at : at + P],
+                        lhsT=source[:, fb, col * P : (col + 1) * P],
                         rhs=ident[:],
                         is_transpose=True,
-                        start=(i == 0),
-                        stop=(i == len(taps) - 1),
+                        start=(i == 0 and fb == 0),
+                        stop=(i == len(parts) - 1 and fb == F_BLOCKS - 1),
                     )
             group = c // CHUNK_COLS
             if c % CHUNK_COLS == 0:

@@ -34,6 +34,7 @@ LOAD_BUFS = 6
 AHEAD = 2
 STEP = 2
 LAG = 8
+ISSUES = 2
 
 D9 = (9.0 + EPS_DEG) ** -0.5
 D6 = (6.0 + EPS_DEG) ** -0.5
@@ -143,19 +144,20 @@ def tile_graphconvolutionbatch_kernel(tc, H, W, gamma, beta, out):
         h_scales = const.tile([P, NODES], U8, align_bytes=64)
         stats = const.tile([P, F_BLOCKS, N_CHUNKS, 6], F32)
 
-        def multiply(chunk, fb):
+        def multiply(chunk, fb, issues=1):
             nodes = slice(chunk * CHUNK, (chunk + 1) * CHUNK)
             feats = slice(fb * P, (fb + 1) * P)
             y = psum.tile([P, CHUNK], F32, tag="y")
-            nc.tensor.matmul_mx(
-                out=y[:],
-                lhsT=w_codes[:, feats].bitcast(FP8X4),
-                lhsT_scale=w_scales[:, feats],
-                rhs=h_codes[:, nodes].bitcast(FP8X4),
-                rhs_scale=h_scales[:, nodes],
-                start=True,
-                stop=True,
-            )
+            for issue in range(issues):
+                nc.tensor.matmul_mx(
+                    out=y[:],
+                    lhsT=w_codes[:, feats].bitcast(FP8X4),
+                    lhsT_scale=w_scales[:, feats],
+                    rhs=h_codes[:, nodes].bitcast(FP8X4),
+                    rhs_scale=h_scales[:, nodes],
+                    start=True,
+                    stop=True,
+                )
             return y
 
         def turn(chunk):
@@ -221,7 +223,7 @@ def tile_graphconvolutionbatch_kernel(tc, H, W, gamma, beta, out):
 
         def norm_relu(chunk, fb):
             pad_tile = padded[chunk % N_PADDED]
-            y = multiply(chunk, fb)
+            y = multiply(chunk, fb, issues=ISSUES)
             y_runs = y[:].rearrange("p (q r) -> p q r", r=ROWS)
             for first, count, on_edge in column_runs(chunk):
                 coeff = edge if on_edge else inner

@@ -34,7 +34,7 @@ LOAD_BUFS = 6
 AHEAD = 2
 STEP = 2
 LAG = 8
-ISSUES = 2
+VECTOR_COLUMN = 1
 
 D9 = (9.0 + EPS_DEG) ** -0.5
 D6 = (6.0 + EPS_DEG) ** -0.5
@@ -49,6 +49,10 @@ def column_runs(chunk):
     if chunk == N_CHUNKS - 1:
         return [(0, CHUNK_COLS - 1, False), (CHUNK_COLS - 1, 1, True)]
     return [(0, CHUNK_COLS, False)]
+
+
+def half_of(count, half):
+    return slice(half * count // 2, (half + 1) * count // 2)
 
 
 def tile_graphconvolutionbatch_kernel(tc, H, W, gamma, beta, out):
@@ -144,20 +148,19 @@ def tile_graphconvolutionbatch_kernel(tc, H, W, gamma, beta, out):
         h_scales = const.tile([P, NODES], U8, align_bytes=64)
         stats = const.tile([P, F_BLOCKS, N_CHUNKS, 6], F32)
 
-        def multiply(chunk, fb, issues=1):
+        def multiply(chunk, fb):
             nodes = slice(chunk * CHUNK, (chunk + 1) * CHUNK)
             feats = slice(fb * P, (fb + 1) * P)
             y = psum.tile([P, CHUNK], F32, tag="y")
-            for issue in range(issues):
-                nc.tensor.matmul_mx(
-                    out=y[:],
-                    lhsT=w_codes[:, feats].bitcast(FP8X4),
-                    lhsT_scale=w_scales[:, feats],
-                    rhs=h_codes[:, nodes].bitcast(FP8X4),
-                    rhs_scale=h_scales[:, nodes],
-                    start=True,
-                    stop=True,
-                )
+            nc.tensor.matmul_mx(
+                out=y[:],
+                lhsT=w_codes[:, feats].bitcast(FP8X4),
+                lhsT_scale=w_scales[:, feats],
+                rhs=h_codes[:, nodes].bitcast(FP8X4),
+                rhs_scale=h_scales[:, nodes],
+                start=True,
+                stop=True,
+            )
             return y
 
         def turn(chunk):
@@ -223,7 +226,7 @@ def tile_graphconvolutionbatch_kernel(tc, H, W, gamma, beta, out):
 
         def norm_relu(chunk, fb):
             pad_tile = padded[chunk % N_PADDED]
-            y = multiply(chunk, fb, issues=ISSUES)
+            y = multiply(chunk, fb)
             y_runs = y[:].rearrange("p (q r) -> p q r", r=ROWS)
             for first, count, on_edge in column_runs(chunk):
                 coeff = edge if on_edge else inner
@@ -237,33 +240,45 @@ def tile_graphconvolutionbatch_kernel(tc, H, W, gamma, beta, out):
 
         def sum_over_rows(chunk):
             pad_tile = padded[chunk % N_PADDED]
+            n_runs = F_BLOCKS * RUNS
             by_block = pad_tile[:].rearrange("p (f q) s -> p f q s", f=F_BLOCKS)
-            for first, count, on_edge in column_runs(chunk):
-                ends = by_block[:, :, BATCH * first : BATCH * (first + count), EVEN_AT - 1 : EVEN_AT + 1]
-                nc.vector.tensor_scalar_mul(out=ends, in0=ends, scalar1=(D4 / D6 if on_edge else D6 / D9))
-            both = halves.tile([P, F_BLOCKS * RUNS, HALF], F32, name="both")
-            nc.vector.tensor_add(
-                out=both[:],
-                in0=pad_tile[:, :, EVEN_AT : EVEN_AT + HALF],
-                in1=pad_tile[:, :, ODD_AT : ODD_AT + HALF],
-            )
+            for half in range(2):
+                for first, count, on_edge in column_runs(chunk):
+                    ends = by_block[
+                        :, half_of(F_BLOCKS, half), BATCH * first : BATCH * (first + count), EVEN_AT - 1 : EVEN_AT + 1
+                    ]
+                    nc.vector.tensor_scalar_mul(out=ends, in0=ends, scalar1=(D4 / D6 if on_edge else D6 / D9))
+            both = halves.tile([P, n_runs, HALF], F32, name="both")
+            for half in range(2):
+                runs = half_of(n_runs, half)
+                nc.vector.tensor_add(
+                    out=both[:, runs, :],
+                    in0=pad_tile[:, runs, EVEN_AT : EVEN_AT + HALF],
+                    in1=pad_tile[:, runs, ODD_AT : ODD_AT + HALF],
+                )
             outer = (
                 pad_tile[:, :, ODD_AT - 1 : ODD_AT - 1 + 2 * (HALF + 2)]
                 .rearrange("p g (t w) -> p g t w", t=2)[:, :, :, 0:HALF]
                 .rearrange("p g t k -> p g k t")
             )
             total = sums.tile([P, F_BLOCKS, CHUNK], F32, name="total")
-            nc.vector.tensor_add(
-                out=total[:].rearrange("p f (q k t) -> p (f q) k t", k=HALF, t=2),
-                in0=both[:].unsqueeze(3).to_broadcast([P, F_BLOCKS * RUNS, HALF, 2]),
-                in1=outer,
-            )
+            total_runs = total[:].rearrange("p f (q k t) -> p (f q) k t", k=HALF, t=2)
+            for half in range(2):
+                runs = half_of(n_runs, half)
+                nc.vector.tensor_add(
+                    out=total_runs[:, runs, :, :],
+                    in0=both[:, runs, :].unsqueeze(3).to_broadcast([P, n_runs // 2, HALF, 2]),
+                    in1=outer[:, runs, :, :],
+                )
             row_sums[chunk] = total
             pair = pairs.tile([P, F_BLOCKS, CHUNK // 2], F32, name="pair")
+            pair_columns = pair[:].rearrange("p f (e n) -> p (f e) n", n=P)
             columns = total[:].rearrange("p f (e two n) -> p (f e) two n", two=2, n=P)
-            nc.vector.tensor_add(
-                out=pair[:].rearrange("p f (e n) -> p (f e) n", n=P), in0=columns[:, :, 0, :], in1=columns[:, :, 1, :]
-            )
+            for half in range(2):
+                some = half_of(F_BLOCKS * CHUNK_COLS // 2, half)
+                nc.vector.tensor_add(
+                    out=pair_columns[:, some, :], in0=columns[:, some, 0, :], in1=columns[:, some, 1, :]
+                )
             pair_sums[chunk] = pair
 
         def finish_column(c):
@@ -285,12 +300,17 @@ def tile_graphconvolutionbatch_kernel(tc, H, W, gamma, beta, out):
             group = c // CHUNK_COLS
             if c % CHUNK_COLS == 0:
                 results[group] = stores.tile([P, CHUNK_COLS, OUT_DIM], F32, name="result")
-            nc.scalar.activation(
-                out=results[group][:, c % CHUNK_COLS, :],
-                in_=turned_back[:],
-                func=ACT.Copy,
-                scale=d_out[:, c : c + 1],
-            )
+            if c % CHUNK_COLS == VECTOR_COLUMN:
+                nc.vector.tensor_scalar_mul(
+                    out=results[group][:, c % CHUNK_COLS, :], in0=turned_back[:], scalar1=d_out[:, c : c + 1]
+                )
+            else:
+                nc.scalar.activation(
+                    out=results[group][:, c % CHUNK_COLS, :],
+                    in_=turned_back[:],
+                    func=ACT.Copy,
+                    scale=d_out[:, c : c + 1],
+                )
             if c % CHUNK_COLS == CHUNK_COLS - 1:
                 nc.sync.dma_start(
                     out=out_view[:, group * CHUNK_COLS : (group + 1) * CHUNK_COLS, :], in_=results[group][:]

from contextlib import ExitStack

import concourse.mybir as mybir
from concourse.masks import make_identity

F32 = mybir.dt.float32
BF16 = mybir.dt.bfloat16
U32 = mybir.dt.uint32
U8 = mybir.dt.uint8
FP8X4 = mybir.dt.float8_e4m3fn_x4
ACT = mybir.ActivationFunctionType
ALU = mybir.AluOpType
AXIS = mybir.AxisListType

P = 128
BATCH, ROWS, COLS = 2, 64, 64
IN_DIM, OUT_DIM = 512, 512
NODES = BATCH * ROWS * COLS
EPS_BN = 1e-5
EPS_DEG = 1e-5

PACK = 4
F_BLOCKS = OUT_DIM // P
CHUNK_COLS = 4
CHUNK = CHUNK_COLS * P
N_CHUNKS = COLS // CHUNK_COLS
RUNS = CHUNK // ROWS
HALF = ROWS // 2
PITCH = 72
ODD_AT = 4
EVEN_AT = ODD_AT + HALF
N_PADDED = 3
LOAD_BUFS = 6
AHEAD = 2
STEP = 2
LAG = 8
VECTOR_COLUMN = 1

D9 = (9.0 + EPS_DEG) ** -0.5
D6 = (6.0 + EPS_DEG) ** -0.5
D4 = (4.0 + EPS_DEG) ** -0.5

FLOPS = 2 * NODES * IN_DIM * OUT_DIM


def column_runs(chunk):
    if chunk == 0:
        return [(0, 1, True), (1, CHUNK_COLS - 1, False)]
    if chunk == N_CHUNKS - 1:
        return [(0, CHUNK_COLS - 1, False), (CHUNK_COLS - 1, 1, True)]
    return [(0, CHUNK_COLS, False)]


def half_of(count, half):
    return slice(half * count // 2, (half + 1) * count // 2)


def tile_graphconvolutionbatch_kernel(tc, H, W, gamma, beta, out):
    nc = tc.nc
    h_view = H.rearrange("b (r c) k -> (b r) c k", c=COLS)
    out_view = out.rearrange("b (r c) f -> (b r) c f", c=COLS)

    with ExitStack() as ctx:
        const = ctx.enter_context(tc.tile_pool(name="const", bufs=1))
        loads = ctx.enter_context(tc.tile_pool(name="loads", bufs=LOAD_BUFS))
        stage = ctx.enter_context(tc.tile_pool(name="stage", bufs=3))
        sums = ctx.enter_context(tc.tile_pool(name="sums", bufs=5))
        halves = ctx.enter_context(tc.tile_pool(name="halves", bufs=2))
        pairs = ctx.enter_context(tc.tile_pool(name="pairs", bufs=5))
        stores = ctx.enter_context(tc.tile_pool(name="stores", bufs=3))
        psum = ctx.enter_context(tc.psum_pool(name="psum", bufs=4))

        h_raw = {}

        def load(chunk):
            h_raw[chunk] = loads.tile([P, CHUNK_COLS, IN_DIM], BF16, name="h_raw")
            nc.sync.dma_start(
                out=h_raw[chunk][:], in_=h_view[:, chunk * CHUNK_COLS : (chunk + 1) * CHUNK_COLS, :]
            )

        ident = const.tile([P, P], F32)
        make_identity(nc, ident[:])
        odd_first = const.tile([P, P], F32)
        ident_rows = ident[:].rearrange("p (b k t) -> p b t k", b=BATCH, t=2)
        odd_first_halves = odd_first[:].rearrange("p (b s k) -> p b s k", b=BATCH, s=2)
        for s in range(2):
            nc.vector.tensor_copy(out=odd_first_halves[:, :, s, :], in_=ident_rows[:, :, 1 - s, :])

        w_raw = const.tile([P, PACK, OUT_DIM], BF16)
        for u in range(2):
            nc.sync.dma_start(
                out=w_raw[:, 2 * u : 2 * u + 2, :],
                in_=W[256 * u : 256 * (u + 1), :].rearrange("(q e) f -> q e f", e=2),
            )
        for chunk in range(LOAD_BUFS):
            load(chunk)
        w_grouped = const.tile([P, OUT_DIM, PACK], BF16, align_bytes=64)
        nc.vector.tensor_copy(out=w_grouped[:], in_=w_raw[:].rearrange("p t f -> p f t"))
        w_codes = const.tile([P, OUT_DIM], U32, align_bytes=64)
        w_scales = const.tile([P, OUT_DIM], U8, align_bytes=64)
        nc.vector.quantize_mx(
            out=w_codes[:].bitcast(FP8X4),
            scales=w_scales[:],
            in_=w_grouped[:].rearrange("p f t -> p (f t)"),
        )

        gb_rows = const.tile([P, P], BF16)
        nc.vector.memset(gb_rows[:], 0.0)
        nc.scalar.dma_start(out=gb_rows[0:F_BLOCKS, :], in_=gamma.rearrange("(j p) -> j p", p=P))
        nc.scalar.dma_start(
            out=gb_rows[F_BLOCKS : 2 * F_BLOCKS, :], in_=beta.rearrange("(j p) -> j p", p=P)
        )
        gb_rows_f32 = const.tile([P, P], F32)
        nc.vector.tensor_copy(out=gb_rows_f32[:], in_=gb_rows[:])
        gb_bank = psum.tile([P, P], F32, tag="t")
        nc.tensor.transpose(gb_bank[:], gb_rows_f32[:], ident[:])
        gb = const.tile([P, 2 * F_BLOCKS], F32)
        nc.vector.tensor_copy(out=gb[:], in_=gb_bank[:, 0 : 2 * F_BLOCKS])

        on_row_edge = const.tile([P, 1], F32)
        nc.vector.tensor_reduce(
            out=on_row_edge[:],
            in_=ident[:].rearrange("p (b r) -> p b r", r=ROWS)[:, :, 0 : ROWS : ROWS - 1],
            axis=AXIS.XY,
            op=ALU.add,
        )
        rows_in_reach = const.tile([P, 1], F32)
        nc.vector.tensor_scalar(
            out=rows_in_reach[:], in0=on_row_edge[:], scalar1=-1.0, scalar2=3.0, op0=ALU.mult, op1=ALU.add
        )
        degree = const.tile([P, COLS], F32)
        nc.vector.memset(degree[:], 3.0)
        nc.vector.memset(degree[:, 0 : COLS : COLS - 1], 2.0)
        nc.vector.tensor_scalar(
            out=degree[:], in0=degree[:], scalar1=rows_in_reach[:, 0:1], scalar2=EPS_DEG, op0=ALU.mult, op1=ALU.add
        )
        nc.scalar.sqrt(out=degree[:], in_=degree[:])
        d_out = const.tile([P, COLS], F32)
        nc.vector.reciprocal(out=d_out[:], in_=degree[:])

        padded = []
        for i in range(N_PADDED):
            pad_tile = const.tile([P, F_BLOCKS * RUNS, PITCH], F32, name="padded%d" % i)
            nc.vector.memset(pad_tile[:, :, ODD_AT - 1 : ODD_AT + ROWS + 1 : ROWS + 1], 0.0)
            padded.append(pad_tile)

        h_codes = const.tile([P, NODES], U32, align_bytes=64)
        h_scales = const.tile([P, NODES], U8, align_bytes=64)
        stats = const.tile([P, F_BLOCKS, N_CHUNKS, 6], F32)

        def multiply(chunk, fb):
            nodes = slice(chunk * CHUNK, (chunk + 1) * CHUNK)
            feats = slice(fb * P, (fb + 1) * P)
            y = psum.tile([P, CHUNK], F32, tag="y")
            nc.tensor.matmul_mx(
                out=y[:],
                lhsT=w_codes[:, feats].bitcast(FP8X4),
                lhsT_scale=w_scales[:, feats],
                rhs=h_codes[:, nodes].bitcast(FP8X4),
                rhs_scale=h_scales[:, nodes],
                start=True,
                stop=True,
            )
            return y

        def turn(chunk):
            grouped = stage.tile([P, CHUNK * PACK], BF16, align_bytes=64, name="grouped")
            grouped_words = grouped[:].bitcast(F32).rearrange("p (n u) -> p n u", u=2)
            for half in range(2):
                turned = psum.tile([P, 2, 2 * P], F32, tag="t", name="turned")
                for i in range(2):
                    words = h_raw[chunk][:, 2 * half + i, :].bitcast(F32)
                    for u in range(2):
                        nc.tensor.transpose(
                            turned[:, u, i * P : (i + 1) * P], words[:, u * P : (u + 1) * P], odd_first[:]
                        )
                nc.scalar.copy(
                    out=grouped_words[:, half * 2 * P : (half + 1) * 2 * P, :],
                    in_=turned[:].rearrange("p u n -> p n u"),
                )
            return grouped

        def quantise(chunk, grouped):
            nodes = slice(chunk * CHUNK, (chunk + 1) * CHUNK)
            nc.vector.quantize_mx(
                out=h_codes[:, nodes].bitcast(FP8X4), scales=h_scales[:, nodes], in_=grouped[:]
            )

        ctx.enter_context(tc.manual_schedule())

        def prepare(chunk):
            quantise(chunk, turn(chunk))
            if chunk + LOAD_BUFS < N_CHUNKS:
                load(chunk + LOAD_BUFS)

        for chunk in range(AHEAD):
            prepare(chunk)
        for chunk in range(N_CHUNKS):
            for fb in range(F_BLOCKS):
                y = multiply(chunk, fb)
                nc.vector.bn_stats(out=stats[:, fb, chunk, :], in_=y[:])
            if chunk + AHEAD < N_CHUNKS:
                prepare(chunk + AHEAD)

        mean_var = const.tile([P, F_BLOCKS, 2], F32)
        for fb in range(F_BLOCKS):
            nc.vector.bn_aggr(out=mean_var[:, fb, :], in_=stats[:, fb, :, :].rearrange("p j s -> p (j s)"))
        std = const.tile([P, F_BLOCKS], F32)
        nc.vector.tensor_scalar_add(out=std[:], in0=mean_var[:, :, 1], scalar1=EPS_BN)
        nc.scalar.sqrt(out=std[:], in_=std[:])
        rstd = const.tile([P, F_BLOCKS], F32)
        nc.vector.reciprocal(out=rstd[:], in_=std[:])
        gain_shift = const.tile([P, 2, F_BLOCKS], F32)
        nc.vector.tensor_mul(out=gain_shift[:, 0, :], in0=gb[:, 0:F_BLOCKS], in1=rstd[:])
        mean_gain = const.tile([P, F_BLOCKS], F32)
        nc.vector.tensor_mul(out=mean_gain[:], in0=mean_var[:, :, 0], in1=gain_shift[:, 0, :])
        nc.vector.tensor_sub(out=gain_shift[:, 1, :], in0=gb[:, F_BLOCKS : 2 * F_BLOCKS], in1=mean_gain[:])
        inner = const.tile([P, 2, F_BLOCKS], F32)
        nc.vector.tensor_scalar_mul(out=inner[:], in0=gain_shift[:], scalar1=D9)
        edge = const.tile([P, 2, F_BLOCKS], F32)
        nc.vector.tensor_scalar_mul(out=edge[:], in0=gain_shift[:], scalar1=D6)

        row_sums = {}
        pair_sums = {}
        results = {}

        def norm_relu(chunk, fb):
            pad_tile = padded[chunk % N_PADDED]
            y = multiply(chunk, fb)
            y_runs = y[:].rearrange("p (q r) -> p q r", r=ROWS)
            for first, count, on_edge in column_runs(chunk):
                coeff = edge if on_edge else inner
                nc.scalar.activation(
                    out=pad_tile[:, fb * RUNS + BATCH * first : fb * RUNS + BATCH * (first + count), ODD_AT : ODD_AT + ROWS],
                    in_=y_runs[:, BATCH * first : BATCH * (first + count), :],
                    func=ACT.Relu,
                    bias=coeff[:, 1, fb : fb + 1],
                    scale=coeff[:, 0, fb : fb + 1],
                )

        def sum_over_rows(chunk):
            pad_tile = padded[chunk % N_PADDED]
            n_runs = F_BLOCKS * RUNS
            by_block = pad_tile[:].rearrange("p (f q) s -> p f q s", f=F_BLOCKS)
            for half in range(2):
                for first, count, on_edge in column_runs(chunk):
                    ends = by_block[
                        :, half_of(F_BLOCKS, half), BATCH * first : BATCH * (first + count), EVEN_AT - 1 : EVEN_AT + 1
                    ]
                    nc.vector.tensor_scalar_mul(out=ends, in0=ends, scalar1=(D4 / D6 if on_edge else D6 / D9))
            both = halves.tile([P, n_runs, HALF], F32, name="both")
            for half in range(2):
                runs = half_of(n_runs, half)
                nc.vector.tensor_add(
                    out=both[:, runs, :],
                    in0=pad_tile[:, runs, EVEN_AT : EVEN_AT + HALF],
                    in1=pad_tile[:, runs, ODD_AT : ODD_AT + HALF],
                )
            outer = (
                pad_tile[:, :, ODD_AT - 1 : ODD_AT - 1 + 2 * (HALF + 2)]
                .rearrange("p g (t w) -> p g t w", t=2)[:, :, :, 0:HALF]
                .rearrange("p g t k -> p g k t")
            )
            total = sums.tile([P, F_BLOCKS, CHUNK], F32, name="total")
            total_runs = total[:].rearrange("p f (q k t) -> p (f q) k t", k=HALF, t=2)
            for half in range(2):
                runs = half_of(n_runs, half)
                nc.vector.tensor_add(
                    out=total_runs[:, runs, :, :],
                    in0=both[:, runs, :].unsqueeze(3).to_broadcast([P, n_runs // 2, HALF, 2]),
                    in1=outer[:, runs, :, :],
                )
            row_sums[chunk] = total
            pair = pairs.tile([P, F_BLOCKS, CHUNK // 2], F32, name="pair")
            pair_columns = pair[:].rearrange("p f (e n) -> p (f e) n", n=P)
            columns = total[:].rearrange("p f (e two n) -> p (f e) two n", two=2, n=P)
            for half in range(2):
                some = half_of(F_BLOCKS * CHUNK_COLS // 2, half)
                nc.vector.tensor_add(
                    out=pair_columns[:, some, :], in0=columns[:, some, 0, :], in1=columns[:, some, 1, :]
                )
            pair_sums[chunk] = pair

        def finish_column(c):
            beyond = c - 1 if c % 2 == 0 else c + 1
            parts = [(pair_sums[c // CHUNK_COLS], (c % CHUNK_COLS) // 2)]
            if 0 <= beyond < COLS:
                parts.append((row_sums[beyond // CHUNK_COLS], beyond % CHUNK_COLS))
            turned_back = psum.tile([P, OUT_DIM], F32, tag="t")
            for i, (source, col) in enumerate(parts):
                for fb in range(F_BLOCKS):
                    nc.tensor.matmul(
                        out=turned_back[:, fb * P : (fb + 1) * P],
                        lhsT=source[:, fb, col * P : (col + 1) * P],
                        rhs=ident[:],
                        is_transpose=True,
                        start=(i == 0 and fb == 0),
                        stop=(i == len(parts) - 1 and fb == F_BLOCKS - 1),
                    )
            group = c // CHUNK_COLS
            if c % CHUNK_COLS == 0:
                results[group] = stores.tile([P, CHUNK_COLS, OUT_DIM], F32, name="result")
            if c % CHUNK_COLS == VECTOR_COLUMN:
                nc.vector.tensor_scalar_mul(
                    out=results[group][:, c % CHUNK_COLS, :], in0=turned_back[:], scalar1=d_out[:, c : c + 1]
                )
            else:
                nc.scalar.activation(
                    out=results[group][:, c % CHUNK_COLS, :],
                    in_=turned_back[:],
                    func=ACT.Copy,
                    scale=d_out[:, c : c + 1],
                )
            if c % CHUNK_COLS == CHUNK_COLS - 1:
                nc.sync.dma_start(
                    out=out_view[:, group * CHUNK_COLS : (group + 1) * CHUNK_COLS, :], in_=results[group][:]
                )

        n_passes = N_CHUNKS * F_BLOCKS
        for first_pass in range(0, n_passes + LAG, STEP):
            for m in range(first_pass, min(first_pass + STEP, n_passes)):
                norm_relu(m // F_BLOCKS, m % F_BLOCKS)
                if m % F_BLOCKS == F_BLOCKS - 1:
                    sum_over_rows(m // F_BLOCKS)
            for c in range(max(first_pass - LAG, 0), min(first_pass - LAG + STEP, COLS)):
                finish_column(c)
